import numpy as np
import ml_dtypes


def mxq(x, axis, fmt="e4m3"):
    dtype, down = {"e4m3": (ml_dtypes.float8_e4m3fn, 7), "e5m2": (ml_dtypes.float8_e5m2, 14)}[fmt]
    v = np.moveaxis(np.asarray(x, np.float32).astype(ml_dtypes.bfloat16).astype(np.float64), axis, -1)
    blocks = v.reshape(v.shape[:-1] + (-1, 32))
    amax = np.abs(blocks).max(-1, keepdims=True)
    byte = np.maximum(np.where(amax > 0, np.frexp(amax)[1] - 1 + 127, 0) - down, 1)
    scale = np.exp2(byte - 127.0)
    codes = (blocks / scale).astype(np.float32).astype(dtype).astype(np.float64)
    return np.moveaxis((codes * scale).reshape(v.shape), -1, axis)


WIDE = False


def mx_kscale(k):
    if not WIDE:
        return np.ones(k)
    levels = np.array([10, -10, 5, -5, 0])
    if k % 512:
        return np.exp2(np.random.permutation(np.resize(levels, k // 32))).repeat(32)
    a = np.empty((k // 512, 16))
    for p in range(k // 512):
        a[p, :8] = np.random.permutation(np.resize(levels, 8))
        for g in range(8):
            far = levels[np.abs(levels - a[p, g]) >= 10]
            a[p, g + 8] = far[np.random.randint(len(far))]
    return np.exp2(a.ravel()).repeat(32)


BF16 = ml_dtypes.bfloat16


def bf(x):
    return np.asarray(x, np.float32).astype(BF16)


def f64(x):
    return np.asarray(x).astype(np.float64)


B, H = 8192, 256
K = 2 * H
G = 4 * H


def sigmoid(v):
    return 1.0 / (1.0 + np.exp(-v))


def setup_inputs():
    s = mx_kscale(K)
    return {"x": bf(np.random.standard_normal((B, H)) * s[:H]),
            "h_prev": bf(np.random.standard_normal((B, H)) * s[H:]),
            "c_prev": bf(np.random.standard_normal((B, H))),
            "is_rnn": bf(np.random.random((B, 1))),
            "W": bf(np.random.standard_normal((K, G)) / np.sqrt(K) / s[:, None]),
            "b": bf(np.random.standard_normal(G) * 0.3)}


def reference(x, h_prev, c_prev, is_rnn, W, b):
    c_prev, m = f64(c_prev), f64(is_rnn)
    xh = np.concatenate([f64(x), f64(h_prev)], axis=1)
    gates = (mxq(xh, 1, "e4m3") @ mxq(f64(W), 0, "e4m3")) + f64(b)
    i = sigmoid(gates[:, :H])
    f = sigmoid(gates[:, H:2 * H])
    g = np.tanh(gates[:, 2 * H:3 * H])
    o = sigmoid(gates[:, 3 * H:])
    c = f * c_prev + i * g
    c = c * m + c_prev * (1.0 - m)
    o = o * m + (1.0 - m)
    return c, o

@@ -1,0 +1,335 @@
+import concourse.mybir as mybir
+from concourse.masks import make_identity
+
+F32 = mybir.dt.float32
+BF16 = mybir.dt.bfloat16
+U32 = mybir.dt.uint32
+U8 = mybir.dt.uint8
+FP8X4 = mybir.dt.float8_e4m3fn_x4
+ACT = mybir.ActivationFunctionType
+ALU = mybir.AluOpType
+
+P = 128
+PACK = 4
+B, H = 8192, 256
+K = 2 * H
+GATE_COLS = 4 * H
+H_CHUNKS = H // P
+ROW_TILES = B // P
+GROUP_TILES = 4
+GROUP_ROWS = GROUP_TILES * P
+GROUPS = ROW_TILES // GROUP_TILES
+HALF_TILES = GROUP_TILES // 2
+HALF_ROWS = HALF_TILES * P
+LOAD_AHEAD = 4
+
+FLOPS = 2 * B * K * GATE_COLS
+
+GATES = (
+    ("f", 1, ACT.Sigmoid, -1.0),
+    ("i", 0, ACT.Sigmoid, 1.0),
+    ("g", 2, ACT.Tanh, 1.0),
+    ("o", 3, ACT.Sigmoid, -1.0),
+)
+
+
+def tile_bag_lstm_pa_t_kernel(tc, x, h_prev, c_prev, is_rnn, W, b, out_0, out_1):
+    nc = tc.nc
+
+    x_view = x.rearrange("(p t) k -> p t k", t=ROW_TILES)
+    h_view = h_prev.rearrange("(p t) k -> p t k", t=ROW_TILES)
+    c_view = c_prev.rearrange("(p t) k -> p t k", t=ROW_TILES)
+    c_out_view = out_0.rearrange("(p t) k -> p t k", t=ROW_TILES)
+    o_out_view = out_1.rearrange("(p t) k -> p t k", t=ROW_TILES)
+
+    with (
+        tc.tile_pool(name="const", bufs=1) as const,
+        tc.tile_pool(name="xh_in", bufs=LOAD_AHEAD) as xh_in,
+        tc.tile_pool(name="c_in", bufs=LOAD_AHEAD + 2) as c_in,
+        tc.tile_pool(name="quant", bufs=2) as quant,
+        tc.tile_pool(name="acts", bufs=2) as acts,
+        tc.tile_pool(name="mids", bufs=2) as mids,
+        tc.tile_pool(name="outs", bufs=3) as outs,
+        tc.psum_pool(name="z_psum", bufs=4) as z_psum,
+        tc.psum_pool(name="xh_psum", bufs=1) as xh_psum,
+        tc.psum_pool(name="ct_psum", bufs=1) as ct_psum,
+        tc.psum_pool(name="back_psum", bufs=2) as back_psum,
+        tc.manual_schedule(),
+    ):
+        xh_sb, c_sb = {}, {}
+        xh_bank, grouped, xh_codes, xh_scales = {}, {}, {}, {}
+        act_sb, ct_bank, fc_sb, ig_sb, delta_sb = {}, {}, {}, {}, {}
+        back_bank = {}
+
+        def in_range(g):
+            return 0 <= g < GROUPS
+
+        ident_f32 = const.tile([P, P], F32)
+        make_identity(nc, ident_f32[:])
+        ident_bf16 = const.tile([P, P], BF16)
+        make_identity(nc, ident_bf16[:])
+
+        n_chunks = GATE_COLS // P
+        b_rows = const.tile([P, P], BF16)
+        nc.vector.memset(b_rows[:], 0.0)
+        nc.scalar.dma_start(out=b_rows[0:n_chunks, :], in_=b.rearrange("(j p) -> j p", p=P))
+        b_cols = ct_psum.tile([P, P], BF16, tag="ct")
+        nc.tensor.transpose(b_cols[:], b_rows[:], ident_bf16[:])
+        bias_pos = const.tile([P, n_chunks], F32)
+        nc.vector.tensor_copy(out=bias_pos[:], in_=b_cols[:, 0:n_chunks])
+        bias_neg = const.tile([P, n_chunks], F32)
+        nc.vector.tensor_scalar_mul(out=bias_neg[:], in0=b_cols[:, 0:n_chunks], scalar1=-1.0)
+
+        m_bf16 = const.tile([P, ROW_TILES], BF16)
+        nc.scalar.dma_start(out=m_bf16[:], in_=is_rnn.rearrange("(p t) o -> p (t o)", t=ROW_TILES))
+        m_pos = const.tile([P, ROW_TILES], F32)
+        nc.vector.tensor_copy(out=m_pos[:], in_=m_bf16[:])
+        m_neg = const.tile([P, ROW_TILES], F32)
+        nc.vector.tensor_scalar_mul(out=m_neg[:], in0=m_bf16[:], scalar1=-1.0)
+
+        w_raw = const.tile([P, PACK, GATE_COLS], BF16)
+        w_grouped = const.tile([P, GATE_COLS, PACK], BF16, align_bytes=64)
+        w_codes = const.tile([P, GATE_COLS], U32, align_bytes=64)
+        w_scales = const.tile([P, GATE_COLS], U8, align_bytes=64)
+
+        def load_weights(first_block):
+            cols = slice(first_block * H, (first_block + 2) * H)
+            nc.sync.dma_start(
+                out=w_raw[:, :, cols], in_=W[:, cols].rearrange("(p t) n -> p t n", t=PACK)
+            )
+
+        def regroup_weights(block, copy):
+            cols = slice(block * H, (block + 1) * H)
+            copy(out=w_grouped[:, cols, :], in_=w_raw[:, :, cols].rearrange("p t n -> p n t"))
+
+        def quantise_weights(block):
+            cols = slice(block * H, (block + 1) * H)
+            nc.vector.quantize_mx(
+                out=w_codes[:, cols].bitcast(FP8X4),
+                scales=w_scales[:, cols],
+                in_=w_grouped[:, cols, :].rearrange("p n t -> p (n t)"),
+            )
+
+        def load_xh(g):
+            if not in_range(g):
+                return
+            tiles = slice(g * GROUP_TILES, (g + 1) * GROUP_TILES)
+            xh_sb[g] = xh_in.tile([P, GROUP_TILES, K], BF16, name="xh_sb")
+            nc.sync.dma_start(out=xh_sb[g][:, :, 0:H], in_=x_view[:, tiles, :])
+            nc.sync.dma_start(out=xh_sb[g][:, :, H:K], in_=h_view[:, tiles, :])
+
+        def load_c(g):
+            if not in_range(g):
+                return
+            tiles = slice(g * GROUP_TILES, (g + 1) * GROUP_TILES)
+            c_sb[g] = c_in.tile([P, GROUP_TILES, H], BF16, name="c_sb")
+            nc.sync.dma_start(out=c_sb[g][:], in_=c_view[:, tiles, :])
+
+        def transpose_xh(g, half):
+            if not in_range(g):
+                return
+            bank = xh_psum.tile([P, 2, HALF_ROWS], F32, name="xh_bank")
+            for u in range(2):
+                for j in range(HALF_TILES):
+                    words = xh_sb[g][:, half * HALF_TILES + j, :].bitcast(F32)
+                    nc.tensor.transpose(
+                        bank[:, u, j * P : (j + 1) * P], words[:, u : K // 2 : 2], ident_f32[:]
+                    )
+            xh_bank[(g, half)] = bank
+
+        def regroup_xh(g, half):
+            if not in_range(g):
+                return
+            if half == 0:
+                grouped[g] = quant.tile([P, GROUP_ROWS * PACK], BF16, name="grouped", align_bytes=64)
+            words = grouped[g][:].bitcast(F32).rearrange("p (r u) -> p r u", u=2)
+            copy = nc.scalar.copy if half == 0 else nc.vector.tensor_copy
+            copy(
+                out=words[:, half * HALF_ROWS : (half + 1) * HALF_ROWS, :],
+                in_=xh_bank[(g, half)][:].rearrange("p u r -> p r u"),
+            )
+
+        def quantise_xh(g):
+            if not in_range(g):
+                return
+            xh_codes[g] = quant.tile([P, GROUP_ROWS], U32, name="xh_codes", align_bytes=64)
+            xh_scales[g] = quant.tile([P, GROUP_ROWS], U8, name="xh_scales", align_bytes=64)
+            nc.vector.quantize_mx(
+                out=xh_codes[g][:].bitcast(FP8X4), scales=xh_scales[g][:], in_=grouped[g][:]
+            )
+
+        def gate(g, which):
+            if not in_range(g):
+                return
+            name, block, func, sign = GATES[which]
+            bias = bias_pos if sign > 0 else bias_neg
+            act_sb[(g, name)] = acts.tile([P, H_CHUNKS, GROUP_ROWS], F32, name="act_" + name)
+            for chunk in range(H_CHUNKS):
+                j = block * H_CHUNKS + chunk
+                z = z_psum.tile([P, GROUP_ROWS], F32, name="z")
+                nc.tensor.matmul_mx(
+                    out=z[:],
+                    lhsT=w_codes[:, j * P : (j + 1) * P].bitcast(FP8X4),
+                    lhsT_scale=w_scales[:, j * P : (j + 1) * P],
+                    rhs=xh_codes[g][:].bitcast(FP8X4),
+                    rhs_scale=xh_scales[g][:],
+                    start=True,
+                    stop=True,
+                )
+                nc.scalar.activation(
+                    out=act_sb[(g, name)][:, chunk, :],
+                    in_=z[:],
+                    func=func,
+                    bias=bias[:, j : j + 1],
+                    scale=sign,
+                )
+
+        def transpose_c(g):
+            if not in_range(g):
+                return
+            bank = ct_psum.tile([P, H_CHUNKS, GROUP_ROWS], BF16, tag="ct", name="ct_bank")
+            for j in range(GROUP_TILES):
+                for chunk in range(H_CHUNKS):
+                    nc.tensor.transpose(
+                        bank[:, chunk, j * P : (j + 1) * P],
+                        c_sb[g][:, j, chunk * P : (chunk + 1) * P],
+                        ident_bf16[:],
+                    )
+            ct_bank[g] = bank
+
+        def forget_product(g):
+            if not in_range(g):
+                return
+            fc_sb[g] = mids.tile([P, H_CHUNKS, GROUP_ROWS], F32, name="fc_sb")
+            nc.vector.tensor_tensor(
+                out=fc_sb[g][:], in0=act_sb[(g, "f")][:], in1=ct_bank[g][:], op=ALU.mult
+            )
+
+        def input_product(g):
+            if not in_range(g):
+                return
+            ig_sb[g] = mids.tile([P, H_CHUNKS, GROUP_ROWS], F32, name="ig_sb")
+            for chunk in range(H_CHUNKS):
+                nc.gpsimd.tensor_tensor(
+                    out=ig_sb[g][:, chunk, :],
+                    in0=act_sb[(g, "i")][:, chunk, :],
+                    in1=act_sb[(g, "g")][:, chunk, :],
+                    op=ALU.mult,
+                )
+
+        def cell_change(g, chunk, engine):
+            if not in_range(g):
+                return
+            if chunk == 0:
+                delta_sb[g] = mids.tile([P, H_CHUNKS, GROUP_ROWS], F32, name="delta_sb")
+            engine.tensor_tensor(
+                out=delta_sb[g][:, chunk, :],
+                in0=ig_sb[g][:, chunk, :],
+                in1=fc_sb[g][:, chunk, :],
+                op=ALU.subtract,
+            )
+
+        def transpose_back(g, key):
+            if not in_range(g):
+                return
+            source = delta_sb[g] if key == "c" else act_sb[(g, "o")]
+            for half in range(2):
+                bank = back_psum.tile([P, HALF_TILES, H], F32, name="back_bank")
+                for j in range(HALF_TILES):
+                    rows = slice((half * HALF_TILES + j) * P, (half * HALF_TILES + j + 1) * P)
+                    for chunk in range(H_CHUNKS):
+                        nc.tensor.transpose(
+                            bank[:, j, chunk * P : (chunk + 1) * P],
+                            source[:, chunk, rows],
+                            ident_f32[:],
+                        )
+                back_bank[(g, key, half)] = bank
+
+        def blend_o(g):
+            if not in_range(g):
+                return
+            result = outs.tile([P, GROUP_TILES, H], F32, name="o_result")
+            for half in range(2):
+                for j in range(half * HALF_TILES, (half + 1) * HALF_TILES):
+                    t = g * GROUP_TILES + j
+                    nc.vector.tensor_scalar(
+                        out=result[:, j, :],
+                        in0=back_bank[(g, "o", half)][:, j % HALF_TILES, :],
+                        scalar1=m_neg[:, t : t + 1],
+                        scalar2=1.0,
+                        op0=ALU.mult,
+                        op1=ALU.add,
+                    )
+            store_group(o_out_view, result, g)
+
+        def blend_c(g):
+            if not in_range(g):
+                return
+            result = outs.tile([P, GROUP_TILES, H], F32, name="c_result")
+            for half in range(2):
+                for j in range(half * HALF_TILES, (half + 1) * HALF_TILES):
+                    t = g * GROUP_TILES + j
+                    nc.vector.scalar_tensor_tensor(
+                        out=result[:, j, :],
+                        in0=back_bank[(g, "c", half)][:, j % HALF_TILES, :],
+                        scalar=m_pos[:, t : t + 1],
+                        in1=c_sb[g][:, j, :],
+                        op0=ALU.mult,
+                        op1=ALU.add,
+                    )
+            store_group(c_out_view, result, g)
+
+        def store_group(out_view, result, g):
+            tiles = slice(g * GROUP_TILES, (g + 1) * GROUP_TILES)
+            nc.sync.dma_start(out=out_view[:, tiles, :], in_=result[:])
+
+        def step(n):
+            load_xh(n + LOAD_AHEAD)
+            load_c(n + LOAD_AHEAD)
+            gate(n, 0)
+            gate(n, 1)
+            quantise_xh(n + 1)
+            cell_change(n - 1, 1, nc.vector)
+            transpose_xh(n + 2, 0)
+            transpose_back(n - 1, "o")
+            transpose_c(n)
+            regroup_xh(n + 2, 0)
+            blend_o(n - 1)
+            forget_product(n)
+            gate(n, 2)
+            gate(n, 3)
+            transpose_xh(n + 2, 1)
+            transpose_back(n - 1, "c")
+            regroup_xh(n + 2, 1)
+            blend_c(n - 1)
+            input_product(n)
+            cell_change(n, 0, nc.gpsimd)
+
+        load_xh(0)
+        load_weights(0)
+        load_xh(1)
+        load_weights(2)
+        load_c(0)
+        load_c(1)
+        for g in range(2, LOAD_AHEAD):
+            load_xh(g)
+            load_c(g)
+        blocks = [block for (name, block, func, sign) in GATES]
+        transpose_xh(0, 0)
+        regroup_xh(0, 0)
+        regroup_weights(blocks[0], nc.vector.tensor_copy)
+        regroup_weights(blocks[1], nc.scalar.copy)
+        transpose_xh(0, 1)
+        regroup_xh(0, 1)
+        quantise_weights(blocks[0])
+        quantise_xh(0)
+        quantise_weights(blocks[1])
+        regroup_weights(blocks[2], nc.vector.tensor_copy)
+        regroup_weights(blocks[3], nc.vector.tensor_copy)
+        quantise_weights(blocks[2])
+        quantise_weights(blocks[3])
+        for half in range(2):
+            transpose_xh(1, half)
+            regroup_xh(1, half)
+        for n in range(GROUPS + 1):
+            step(n)

@@ -64,36 +64,41 @@ def tile_bag_lstm_pa_t_kernel(tc, x, h_prev, c_prev, is_rnn, W, b, out_0, out_1)
         def in_range(g):
             return 0 <= g < GROUPS
 
+        warm = const.tile([P, 2], F32)
+        nc.vector.memset(warm[:], 0.0)
+        n_chunks = GATE_COLS // P
+        b_rows = const.tile([P, P], BF16)
+        nc.vector.memset(b_rows[:], 0.0)
+        nc.scalar.dma_start(out=b_rows[0:n_chunks, :], in_=b.rearrange("(j p) -> j p", p=P))
+        m_bf16 = const.tile([P, ROW_TILES], BF16)
+        nc.scalar.dma_start(out=m_bf16[:], in_=is_rnn.rearrange("(p t) o -> p (t o)", t=ROW_TILES))
+        nc.scalar.activation(out=warm[:, 1:2], in_=warm[:, 0:1], func=ACT.Sigmoid)
+
         ident_f32 = const.tile([P, P], F32)
         make_identity(nc, ident_f32[:])
         ident_bf16 = const.tile([P, P], BF16)
         make_identity(nc, ident_bf16[:])
 
-        n_chunks = GATE_COLS // P
-        b_rows = const.tile([P, P], BF16)
-        nc.vector.memset(b_rows[:], 0.0)
-        nc.scalar.dma_start(out=b_rows[0:n_chunks, :], in_=b.rearrange("(j p) -> j p", p=P))
         b_cols = ct_psum.tile([P, P], BF16, tag="ct")
         nc.tensor.transpose(b_cols[:], b_rows[:], ident_bf16[:])
         bias_pos = const.tile([P, n_chunks], F32)
-        nc.vector.tensor_copy(out=bias_pos[:], in_=b_cols[:, 0:n_chunks])
         bias_neg = const.tile([P, n_chunks], F32)
-        nc.vector.tensor_scalar_mul(out=bias_neg[:], in0=b_cols[:, 0:n_chunks], scalar1=-1.0)
-
-        m_bf16 = const.tile([P, ROW_TILES], BF16)
-        nc.scalar.dma_start(out=m_bf16[:], in_=is_rnn.rearrange("(p t) o -> p (t o)", t=ROW_TILES))
         m_pos = const.tile([P, ROW_TILES], F32)
-        nc.vector.tensor_copy(out=m_pos[:], in_=m_bf16[:])
         m_neg = const.tile([P, ROW_TILES], F32)
-        nc.vector.tensor_scalar_mul(out=m_neg[:], in0=m_bf16[:], scalar1=-1.0)
+
+        def convert_constants():
+            nc.vector.tensor_copy(out=bias_pos[:], in_=b_cols[:, 0:n_chunks])
+            nc.vector.tensor_scalar_mul(out=bias_neg[:], in0=b_cols[:, 0:n_chunks], scalar1=-1.0)
+            nc.vector.tensor_copy(out=m_pos[:], in_=m_bf16[:])
+            nc.vector.tensor_scalar_mul(out=m_neg[:], in0=m_bf16[:], scalar1=-1.0)
 
         w_raw = const.tile([P, PACK, GATE_COLS], BF16)
         w_grouped = const.tile([P, GATE_COLS, PACK], BF16, align_bytes=64)
         w_codes = const.tile([P, GATE_COLS], U32, align_bytes=64)
         w_scales = const.tile([P, GATE_COLS], U8, align_bytes=64)
 
-        def load_weights(first_block):
-            cols = slice(first_block * H, (first_block + 2) * H)
+        def load_weights(block):
+            cols = slice(block * H, (block + 1) * H)
             nc.sync.dma_start(
                 out=w_raw[:, :, cols], in_=W[:, cols].rearrange("(p t) n -> p t n", t=PACK)
             )
@@ -125,10 +130,10 @@ def tile_bag_lstm_pa_t_kernel(tc, x, h_prev, c_prev, is_rnn, W, b, out_0, out_1)
             c_sb[g] = c_in.tile([P, GROUP_TILES, H], BF16, name="c_sb")
             nc.sync.dma_start(out=c_sb[g][:], in_=c_view[:, tiles, :])
 
-        def transpose_xh(g, half):
+        def transpose_xh(g, half, pool=xh_psum, tag="xh_bank"):
             if not in_range(g):
                 return
-            bank = xh_psum.tile([P, 2, HALF_ROWS], F32, name="xh_bank")
+            bank = pool.tile([P, 2, HALF_ROWS], F32, name=tag)
             for u in range(2):
                 for j in range(HALF_TILES):
                     words = xh_sb[g][:, half * HALF_TILES + j, :].bitcast(F32)
@@ -137,13 +142,13 @@ def tile_bag_lstm_pa_t_kernel(tc, x, h_prev, c_prev, is_rnn, W, b, out_0, out_1)
                     )
             xh_bank[(g, half)] = bank
 
-        def regroup_xh(g, half):
+        def regroup_xh(g, half, copy=None):
             if not in_range(g):
                 return
             if half == 0:
                 grouped[g] = quant.tile([P, GROUP_ROWS * PACK], BF16, name="grouped", align_bytes=64)
             words = grouped[g][:].bitcast(F32).rearrange("p (r u) -> p r u", u=2)
-            copy = nc.scalar.copy if half == 0 else nc.vector.tensor_copy
+            copy = copy or (nc.scalar.copy if half == 0 else nc.vector.tensor_copy)
             copy(
                 out=words[:, half * HALF_ROWS : (half + 1) * HALF_ROWS, :],
                 in_=xh_bank[(g, half)][:].rearrange("p u r -> p r u"),
@@ -288,16 +293,25 @@ def tile_bag_lstm_pa_t_kernel(tc, x, h_prev, c_prev, is_rnn, W, b, out_0, out_1)
             load_c(n + LOAD_AHEAD)
             gate(n, 0)
             gate(n, 1)
+            if n == 0:
+                for block in blocks[2:]:
+                    regroup_weights(block, nc.vector.tensor_copy)
+                    quantise_weights(block)
             quantise_xh(n + 1)
             cell_change(n - 1, 1, nc.vector)
-            transpose_xh(n + 2, 0)
+            if n > 0:
+                transpose_xh(n + 2, 0)
             transpose_back(n - 1, "o")
             transpose_c(n)
-            regroup_xh(n + 2, 0)
+            if n > 0:
+                regroup_xh(n + 2, 0)
             blend_o(n - 1)
             forget_product(n)
             gate(n, 2)
             gate(n, 3)
+            if n == 0:
+                transpose_xh(n + 2, 0, back_psum, "back_bank")
+                regroup_xh(n + 2, 0, nc.vector.tensor_copy)
             transpose_xh(n + 2, 1)
             transpose_back(n - 1, "c")
             regroup_xh(n + 2, 1)
@@ -305,31 +319,26 @@ def tile_bag_lstm_pa_t_kernel(tc, x, h_prev, c_prev, is_rnn, W, b, out_0, out_1)
             input_product(n)
             cell_change(n, 0, nc.gpsimd)
 
+        blocks = [block for (name, block, func, sign) in GATES]
         load_xh(0)
-        load_weights(0)
+        load_weights(blocks[0])
         load_xh(1)
-        load_weights(2)
+        for block in blocks[1:]:
+            load_weights(block)
         load_c(0)
-        load_c(1)
         for g in range(2, LOAD_AHEAD):
             load_xh(g)
-            load_c(g)
-        blocks = [block for (name, block, func, sign) in GATES]
-        transpose_xh(0, 0)
-        regroup_xh(0, 0)
+            load_c(g - 1)
+        load_c(LOAD_AHEAD - 1)
+        for g in range(2):
+            for half in range(2):
+                transpose_xh(g, half, z_psum, "z")
+                regroup_xh(g, half, nc.scalar.copy)
         regroup_weights(blocks[0], nc.vector.tensor_copy)
-        regroup_weights(blocks[1], nc.scalar.copy)
-        transpose_xh(0, 1)
-        regroup_xh(0, 1)
         quantise_weights(blocks[0])
+        convert_constants()
         quantise_xh(0)
+        regroup_weights(blocks[1], nc.vector.tensor_copy)
         quantise_weights(blocks[1])
-        regroup_weights(blocks[2], nc.vector.tensor_copy)
-        regroup_weights(blocks[3], nc.vector.tensor_copy)
-        quantise_weights(blocks[2])
-        quantise_weights(blocks[3])
-        for half in range(2):
-            transpose_xh(1, half)
-            regroup_xh(1, half)
         for n in range(GROUPS + 1):
             step(n)

@@ -210,12 +210,12 @@ def tile_bag_lstm_pa_t_kernel(tc, x, h_prev, c_prev, is_rnn, W, b, out_0, out_1)
                 out=fc_sb[g][:], in0=act_sb[(g, "f")][:], in1=ct_bank[g][:], op=ALU.mult
             )
 
-        def input_product(g):
+        def input_product(g, engine):
             if not in_range(g):
                 return
             ig_sb[g] = mids.tile([P, H_CHUNKS, GROUP_ROWS], F32, name="ig_sb")
             for chunk in range(H_CHUNKS):
-                nc.gpsimd.tensor_tensor(
+                engine.tensor_tensor(
                     out=ig_sb[g][:, chunk, :],
                     in0=act_sb[(g, "i")][:, chunk, :],
                     in1=act_sb[(g, "g")][:, chunk, :],
@@ -234,12 +234,12 @@ def tile_bag_lstm_pa_t_kernel(tc, x, h_prev, c_prev, is_rnn, W, b, out_0, out_1)
                 op=ALU.subtract,
             )
 
-        def transpose_back(g, key):
+        def transpose_back(g, key, pool=back_psum, tag="back_bank"):
             if not in_range(g):
                 return
             source = delta_sb[g] if key == "c" else act_sb[(g, "o")]
             for half in range(2):
-                bank = back_psum.tile([P, HALF_TILES, H], F32, name="back_bank")
+                bank = pool.tile([P, HALF_TILES, H], F32, name=tag)
                 for j in range(HALF_TILES):
                     rows = slice((half * HALF_TILES + j) * P, (half * HALF_TILES + j + 1) * P)
                     for chunk in range(H_CHUNKS):
@@ -257,15 +257,27 @@ def tile_bag_lstm_pa_t_kernel(tc, x, h_prev, c_prev, is_rnn, W, b, out_0, out_1)
             for half in range(2):
                 for j in range(half * HALF_TILES, (half + 1) * HALF_TILES):
                     t = g * GROUP_TILES + j
-                    nc.vector.tensor_scalar(
-                        out=result[:, j, :],
-                        in0=back_bank[(g, "o", half)][:, j % HALF_TILES, :],
-                        scalar1=m_neg[:, t : t + 1],
-                        scalar2=1.0,
-                        op0=ALU.mult,
-                        op1=ALU.add,
-                    )
-            store_group(o_out_view, result, g)
+                    if g == GROUPS - 1:
+                        nc.scalar.activation(
+                            out=result[:, j, :],
+                            in_=back_bank[(g, "o", half)][:, j % HALF_TILES, :],
+                            func=ACT.Copy,
+                            scale=m_neg[:, t : t + 1],
+                            bias=1.0,
+                        )
+                    else:
+                        nc.vector.tensor_scalar(
+                            out=result[:, j, :],
+                            in0=back_bank[(g, "o", half)][:, j % HALF_TILES, :],
+                            scalar1=m_neg[:, t : t + 1],
+                            scalar2=1.0,
+                            op0=ALU.mult,
+                            op1=ALU.add,
+                        )
+                if g == GROUPS - 1:
+                    store_half(o_out_view, result, g, half, nc.scalar)
+            if g < GROUPS - 1:
+                store_group(o_out_view, result, g)
 
         def blend_c(g):
             if not in_range(g):
@@ -282,11 +294,19 @@ def tile_bag_lstm_pa_t_kernel(tc, x, h_prev, c_prev, is_rnn, W, b, out_0, out_1)
                         op0=ALU.mult,
                         op1=ALU.add,
                     )
-            store_group(c_out_view, result, g)
+                if g == GROUPS - 1:
+                    store_half(c_out_view, result, g, half, nc.sync)
+            if g < GROUPS - 1:
+                store_group(c_out_view, result, g)
 
         def store_group(out_view, result, g):
             tiles = slice(g * GROUP_TILES, (g + 1) * GROUP_TILES)
             nc.sync.dma_start(out=out_view[:, tiles, :], in_=result[:])
+
+        def store_half(out_view, result, g, half, queue):
+            j = slice(half * HALF_TILES, (half + 1) * HALF_TILES)
+            tiles = slice(g * GROUP_TILES + j.start, g * GROUP_TILES + j.stop)
+            queue.dma_start(out=out_view[:, tiles, :], in_=result[:, j, :])
 
         def step(n):
             load_xh(n + LOAD_AHEAD)
@@ -316,8 +336,28 @@ def tile_bag_lstm_pa_t_kernel(tc, x, h_prev, c_prev, is_rnn, W, b, out_0, out_1)
             transpose_back(n - 1, "c")
             regroup_xh(n + 2, 1)
             blend_c(n - 1)
-            input_product(n)
+            input_product(n, nc.gpsimd)
             cell_change(n, 0, nc.gpsimd)
+
+        def last_turn(n):
+            gate(n, 0)
+            gate(n, 1)
+            transpose_c(n)
+            transpose_back(n - 1, "o")
+            forget_product(n)
+            cell_change(n - 1, 1, nc.vector)
+            blend_o(n - 1)
+            gate(n, 2)
+            gate(n, 3)
+            input_product(n, nc.gpsimd)
+            transpose_back(n - 1, "c")
+            blend_c(n - 1)
+            cell_change(n, 0, nc.vector)
+            cell_change(n, 1, nc.vector)
+            transpose_back(n, "o", z_psum, "z")
+            transpose_back(n, "c")
+            blend_o(n)
+            blend_c(n)
 
         blocks = [block for (name, block, func, sign) in GATES]
         load_xh(0)
@@ -340,5 +380,6 @@ def tile_bag_lstm_pa_t_kernel(tc, x, h_prev, c_prev, is_rnn, W, b, out_0, out_1)
         quantise_xh(0)
         regroup_weights(blocks[1], nc.vector.tensor_copy)
         quantise_weights(blocks[1])
-        for n in range(GROUPS + 1):
+        for n in range(GROUPS - 1):
             step(n)
+        last_turn(GROUPS - 1)

import concourse.mybir as mybir
from concourse.masks import make_identity

F32 = mybir.dt.float32
BF16 = mybir.dt.bfloat16
U32 = mybir.dt.uint32
U8 = mybir.dt.uint8
FP8X4 = mybir.dt.float8_e4m3fn_x4
ACT = mybir.ActivationFunctionType
ALU = mybir.AluOpType

P = 128
PACK = 4
B, H = 8192, 256
K = 2 * H
GATE_COLS = 4 * H
H_CHUNKS = H // P
ROW_TILES = B // P
GROUP_TILES = 4
GROUP_ROWS = GROUP_TILES * P
GROUPS = ROW_TILES // GROUP_TILES
HALF_TILES = GROUP_TILES // 2
HALF_ROWS = HALF_TILES * P
LOAD_AHEAD = 4

FLOPS = 2 * B * K * GATE_COLS

GATES = (
    ("f", 1, ACT.Sigmoid, -1.0),
    ("i", 0, ACT.Sigmoid, 1.0),
    ("g", 2, ACT.Tanh, 1.0),
    ("o", 3, ACT.Sigmoid, -1.0),
)


def tile_bag_lstm_pa_t_kernel(tc, x, h_prev, c_prev, is_rnn, W, b, out_0, out_1):
    nc = tc.nc

    x_view = x.rearrange("(p t) k -> p t k", t=ROW_TILES)
    h_view = h_prev.rearrange("(p t) k -> p t k", t=ROW_TILES)
    c_view = c_prev.rearrange("(p t) k -> p t k", t=ROW_TILES)
    c_out_view = out_0.rearrange("(p t) k -> p t k", t=ROW_TILES)
    o_out_view = out_1.rearrange("(p t) k -> p t k", t=ROW_TILES)

    with (
        tc.tile_pool(name="const", bufs=1) as const,
        tc.tile_pool(name="xh_in", bufs=LOAD_AHEAD) as xh_in,
        tc.tile_pool(name="c_in", bufs=LOAD_AHEAD + 2) as c_in,
        tc.tile_pool(name="quant", bufs=2) as quant,
        tc.tile_pool(name="acts", bufs=2) as acts,
        tc.tile_pool(name="mids", bufs=2) as mids,
        tc.tile_pool(name="outs", bufs=3) as outs,
        tc.psum_pool(name="z_psum", bufs=4) as z_psum,
        tc.psum_pool(name="xh_psum", bufs=1) as xh_psum,
        tc.psum_pool(name="ct_psum", bufs=1) as ct_psum,
        tc.psum_pool(name="back_psum", bufs=2) as back_psum,
        tc.manual_schedule(),
    ):
        xh_sb, c_sb = {}, {}
        xh_bank, grouped, xh_codes, xh_scales = {}, {}, {}, {}
        act_sb, ct_bank, fc_sb, ig_sb, delta_sb = {}, {}, {}, {}, {}
        back_bank = {}

        def in_range(g):
            return 0 <= g < GROUPS

        warm = const.tile([P, 2], F32)
        nc.vector.memset(warm[:], 0.0)
        n_chunks = GATE_COLS // P
        b_rows = const.tile([P, P], BF16)
        nc.vector.memset(b_rows[:], 0.0)
        nc.scalar.dma_start(out=b_rows[0:n_chunks, :], in_=b.rearrange("(j p) -> j p", p=P))
        m_bf16 = const.tile([P, ROW_TILES], BF16)
        nc.scalar.dma_start(out=m_bf16[:], in_=is_rnn.rearrange("(p t) o -> p (t o)", t=ROW_TILES))
        nc.scalar.activation(out=warm[:, 1:2], in_=warm[:, 0:1], func=ACT.Sigmoid)

        ident_f32 = const.tile([P, P], F32)
        make_identity(nc, ident_f32[:])
        ident_bf16 = const.tile([P, P], BF16)
        make_identity(nc, ident_bf16[:])

        b_cols = ct_psum.tile([P, P], BF16, tag="ct")
        nc.tensor.transpose(b_cols[:], b_rows[:], ident_bf16[:])
        bias_pos = const.tile([P, n_chunks], F32)
        bias_neg = const.tile([P, n_chunks], F32)
        m_pos = const.tile([P, ROW_TILES], F32)
        m_neg = const.tile([P, ROW_TILES], F32)

        def convert_constants():
            nc.vector.tensor_copy(out=bias_pos[:], in_=b_cols[:, 0:n_chunks])
            nc.vector.tensor_scalar_mul(out=bias_neg[:], in0=b_cols[:, 0:n_chunks], scalar1=-1.0)
            nc.vector.tensor_copy(out=m_pos[:], in_=m_bf16[:])
            nc.vector.tensor_scalar_mul(out=m_neg[:], in0=m_bf16[:], scalar1=-1.0)

        w_raw = const.tile([P, PACK, GATE_COLS], BF16)
        w_grouped = const.tile([P, GATE_COLS, PACK], BF16, align_bytes=64)
        w_codes = const.tile([P, GATE_COLS], U32, align_bytes=64)
        w_scales = const.tile([P, GATE_COLS], U8, align_bytes=64)

        def load_weights(block):
            cols = slice(block * H, (block + 1) * H)
            nc.sync.dma_start(
                out=w_raw[:, :, cols], in_=W[:, cols].rearrange("(p t) n -> p t n", t=PACK)
            )

        def regroup_weights(block, copy):
            cols = slice(block * H, (block + 1) * H)
            copy(out=w_grouped[:, cols, :], in_=w_raw[:, :, cols].rearrange("p t n -> p n t"))

        def quantise_weights(block):
            cols = slice(block * H, (block + 1) * H)
            nc.vector.quantize_mx(
                out=w_codes[:, cols].bitcast(FP8X4),
                scales=w_scales[:, cols],
                in_=w_grouped[:, cols, :].rearrange("p n t -> p (n t)"),
            )

        def load_xh(g):
            if not in_range(g):
                return
            tiles = slice(g * GROUP_TILES, (g + 1) * GROUP_TILES)
            xh_sb[g] = xh_in.tile([P, GROUP_TILES, K], BF16, name="xh_sb")
            nc.sync.dma_start(out=xh_sb[g][:, :, 0:H], in_=x_view[:, tiles, :])
            nc.sync.dma_start(out=xh_sb[g][:, :, H:K], in_=h_view[:, tiles, :])

        def load_c(g):
            if not in_range(g):
                return
            tiles = slice(g * GROUP_TILES, (g + 1) * GROUP_TILES)
            c_sb[g] = c_in.tile([P, GROUP_TILES, H], BF16, name="c_sb")
            nc.sync.dma_start(out=c_sb[g][:], in_=c_view[:, tiles, :])

        def transpose_xh(g, half, pool=xh_psum, tag="xh_bank"):
            if not in_range(g):
                return
            bank = pool.tile([P, 2, HALF_ROWS], F32, name=tag)
            for u in range(2):
                for j in range(HALF_TILES):
                    words = xh_sb[g][:, half * HALF_TILES + j, :].bitcast(F32)
                    nc.tensor.transpose(
                        bank[:, u, j * P : (j + 1) * P], words[:, u : K // 2 : 2], ident_f32[:]
                    )
            xh_bank[(g, half)] = bank

        def regroup_xh(g, half, copy=None):
            if not in_range(g):
                return
            if half == 0:
                grouped[g] = quant.tile([P, GROUP_ROWS * PACK], BF16, name="grouped", align_bytes=64)
            words = grouped[g][:].bitcast(F32).rearrange("p (r u) -> p r u", u=2)
            copy = copy or (nc.scalar.copy if half == 0 else nc.vector.tensor_copy)
            copy(
                out=words[:, half * HALF_ROWS : (half + 1) * HALF_ROWS, :],
                in_=xh_bank[(g, half)][:].rearrange("p u r -> p r u"),
            )

        def quantise_xh(g):
            if not in_range(g):
                return
            xh_codes[g] = quant.tile([P, GROUP_ROWS], U32, name="xh_codes", align_bytes=64)
            xh_scales[g] = quant.tile([P, GROUP_ROWS], U8, name="xh_scales", align_bytes=64)
            nc.vector.quantize_mx(
                out=xh_codes[g][:].bitcast(FP8X4), scales=xh_scales[g][:], in_=grouped[g][:]
            )

        def gate(g, which):
            if not in_range(g):
                return
            name, block, func, sign = GATES[which]
            bias = bias_pos if sign > 0 else bias_neg
            act_sb[(g, name)] = acts.tile([P, H_CHUNKS, GROUP_ROWS], F32, name="act_" + name)
            for chunk in range(H_CHUNKS):
                j = block * H_CHUNKS + chunk
                z = z_psum.tile([P, GROUP_ROWS], F32, name="z")
                nc.tensor.matmul_mx(
                    out=z[:],
                    lhsT=w_codes[:, j * P : (j + 1) * P].bitcast(FP8X4),
                    lhsT_scale=w_scales[:, j * P : (j + 1) * P],
                    rhs=xh_codes[g][:].bitcast(FP8X4),
                    rhs_scale=xh_scales[g][:],
                    start=True,
                    stop=True,
                )
                nc.scalar.activation(
                    out=act_sb[(g, name)][:, chunk, :],
                    in_=z[:],
                    func=func,
                    bias=bias[:, j : j + 1],
                    scale=sign,
                )

        def transpose_c(g):
            if not in_range(g):
                return
            bank = ct_psum.tile([P, H_CHUNKS, GROUP_ROWS], BF16, tag="ct", name="ct_bank")
            for j in range(GROUP_TILES):
                for chunk in range(H_CHUNKS):
                    nc.tensor.transpose(
                        bank[:, chunk, j * P : (j + 1) * P],
                        c_sb[g][:, j, chunk * P : (chunk + 1) * P],
                        ident_bf16[:],
                    )
            ct_bank[g] = bank

        def forget_product(g):
            if not in_range(g):
                return
            fc_sb[g] = mids.tile([P, H_CHUNKS, GROUP_ROWS], F32, name="fc_sb")
            nc.vector.tensor_tensor(
                out=fc_sb[g][:], in0=act_sb[(g, "f")][:], in1=ct_bank[g][:], op=ALU.mult
            )

        def input_product(g, engine):
            if not in_range(g):
                return
            ig_sb[g] = mids.tile([P, H_CHUNKS, GROUP_ROWS], F32, name="ig_sb")
            for chunk in range(H_CHUNKS):
                engine.tensor_tensor(
                    out=ig_sb[g][:, chunk, :],
                    in0=act_sb[(g, "i")][:, chunk, :],
                    in1=act_sb[(g, "g")][:, chunk, :],
                    op=ALU.mult,
                )

        def cell_change(g, chunk, engine):
            if not in_range(g):
                return
            if chunk == 0:
                delta_sb[g] = mids.tile([P, H_CHUNKS, GROUP_ROWS], F32, name="delta_sb")
            engine.tensor_tensor(
                out=delta_sb[g][:, chunk, :],
                in0=ig_sb[g][:, chunk, :],
                in1=fc_sb[g][:, chunk, :],
                op=ALU.subtract,
            )

        def transpose_back(g, key, pool=back_psum, tag="back_bank"):
            if not in_range(g):
                return
            source = delta_sb[g] if key == "c" else act_sb[(g, "o")]
            for half in range(2):
                bank = pool.tile([P, HALF_TILES, H], F32, name=tag)
                for j in range(HALF_TILES):
                    rows = slice((half * HALF_TILES + j) * P, (half * HALF_TILES + j + 1) * P)
                    for chunk in range(H_CHUNKS):
                        nc.tensor.transpose(
                            bank[:, j, chunk * P : (chunk + 1) * P],
                            source[:, chunk, rows],
                            ident_f32[:],
                        )
                back_bank[(g, key, half)] = bank

        def blend_o(g):
            if not in_range(g):
                return
            result = outs.tile([P, GROUP_TILES, H], F32, name="o_result")
            for half in range(2):
                for j in range(half * HALF_TILES, (half + 1) * HALF_TILES):
                    t = g * GROUP_TILES + j
                    if g == GROUPS - 1:
                        nc.scalar.activation(
                            out=result[:, j, :],
                            in_=back_bank[(g, "o", half)][:, j % HALF_TILES, :],
                            func=ACT.Copy,
                            scale=m_neg[:, t : t + 1],
                            bias=1.0,
                        )
                    else:
                        nc.vector.tensor_scalar(
                            out=result[:, j, :],
                            in0=back_bank[(g, "o", half)][:, j % HALF_TILES, :],
                            scalar1=m_neg[:, t : t + 1],
                            scalar2=1.0,
                            op0=ALU.mult,
                            op1=ALU.add,
                        )
                if g == GROUPS - 1:
                    store_half(o_out_view, result, g, half, nc.scalar)
            if g < GROUPS - 1:
                store_group(o_out_view, result, g)

        def blend_c(g):
            if not in_range(g):
                return
            result = outs.tile([P, GROUP_TILES, H], F32, name="c_result")
            for half in range(2):
                for j in range(half * HALF_TILES, (half + 1) * HALF_TILES):
                    t = g * GROUP_TILES + j
                    nc.vector.scalar_tensor_tensor(
                        out=result[:, j, :],
                        in0=back_bank[(g, "c", half)][:, j % HALF_TILES, :],
                        scalar=m_pos[:, t : t + 1],
                        in1=c_sb[g][:, j, :],
                        op0=ALU.mult,
                        op1=ALU.add,
                    )
                if g == GROUPS - 1:
                    store_half(c_out_view, result, g, half, nc.sync)
            if g < GROUPS - 1:
                store_group(c_out_view, result, g)

        def store_group(out_view, result, g):
            tiles = slice(g * GROUP_TILES, (g + 1) * GROUP_TILES)
            nc.sync.dma_start(out=out_view[:, tiles, :], in_=result[:])

        def store_half(out_view, result, g, half, queue):
            j = slice(half * HALF_TILES, (half + 1) * HALF_TILES)
            tiles = slice(g * GROUP_TILES + j.start, g * GROUP_TILES + j.stop)
            queue.dma_start(out=out_view[:, tiles, :], in_=result[:, j, :])

        def step(n):
            load_xh(n + LOAD_AHEAD)
            load_c(n + LOAD_AHEAD)
            gate(n, 0)
            gate(n, 1)
            if n == 0:
                for block in blocks[2:]:
                    regroup_weights(block, nc.vector.tensor_copy)
                    quantise_weights(block)
            quantise_xh(n + 1)
            cell_change(n - 1, 1, nc.vector)
            if n > 0:
                transpose_xh(n + 2, 0)
            transpose_back(n - 1, "o")
            transpose_c(n)
            if n > 0:
                regroup_xh(n + 2, 0)
            blend_o(n - 1)
            forget_product(n)
            gate(n, 2)
            gate(n, 3)
            if n == 0:
                transpose_xh(n + 2, 0, back_psum, "back_bank")
                regroup_xh(n + 2, 0, nc.vector.tensor_copy)
            transpose_xh(n + 2, 1)
            transpose_back(n - 1, "c")
            regroup_xh(n + 2, 1)
            blend_c(n - 1)
            input_product(n, nc.gpsimd)
            cell_change(n, 0, nc.gpsimd)

        def last_turn(n):
            gate(n, 0)
            gate(n, 1)
            transpose_c(n)
            transpose_back(n - 1, "o")
            forget_product(n)
            cell_change(n - 1, 1, nc.vector)
            blend_o(n - 1)
            gate(n, 2)
            gate(n, 3)
            input_product(n, nc.gpsimd)
            transpose_back(n - 1, "c")
            blend_c(n - 1)
            cell_change(n, 0, nc.vector)
            cell_change(n, 1, nc.vector)
            transpose_back(n, "o", z_psum, "z")
            transpose_back(n, "c")
            blend_o(n)
            blend_c(n)

        blocks = [block for (name, block, func, sign) in GATES]
        load_xh(0)
        load_weights(blocks[0])
        load_xh(1)
        for block in blocks[1:]:
            load_weights(block)
        load_c(0)
        for g in range(2, LOAD_AHEAD):
            load_xh(g)
            load_c(g - 1)
        load_c(LOAD_AHEAD - 1)
        for g in range(2):
            for half in range(2):
                transpose_xh(g, half, z_psum, "z")
                regroup_xh(g, half, nc.scalar.copy)
        regroup_weights(blocks[0], nc.vector.tensor_copy)
        quantise_weights(blocks[0])
        convert_constants()
        quantise_xh(0)
        regroup_weights(blocks[1], nc.vector.tensor_copy)
        quantise_weights(blocks[1])
        for n in range(GROUPS - 1):
            step(n)
        last_turn(GROUPS - 1)
